import numpy as np
import ml_dtypes


def mxq(x, axis, fmt="e4m3"):
    dtype, down = {"e4m3": (ml_dtypes.float8_e4m3fn, 7), "e5m2": (ml_dtypes.float8_e5m2, 14)}[fmt]
    v = np.moveaxis(np.asarray(x, np.float32).astype(ml_dtypes.bfloat16).astype(np.float64), axis, -1)
    blocks = v.reshape(v.shape[:-1] + (-1, 32))
    amax = np.abs(blocks).max(-1, keepdims=True)
    byte = np.maximum(np.where(amax > 0, np.frexp(amax)[1] - 1 + 127, 0) - down, 1)
    scale = np.exp2(byte - 127.0)
    codes = (blocks / scale).astype(np.float32).astype(dtype).astype(np.float64)
    return np.moveaxis((codes * scale).reshape(v.shape), -1, axis)


WIDE = False


def mx_kscale(k):
    if not WIDE:
        return np.ones(k)
    levels = np.array([20, -20, 10, -10, 0])
    a = np.random.permutation(np.resize(levels, k // 512 * 4)).reshape(k // 512, 4)
    idx = np.arange(k)
    return np.exp2(a[idx // 512, idx % 128 // 32])


BF16 = ml_dtypes.bfloat16


def bf(x):
    return np.asarray(x, np.float32).astype(BF16)


def f64(x):
    return np.asarray(x).astype(np.float64)


B, T, M, K, N, IN_MATS, OUT_MATS = 2, 256, 8, 16, 32, 32, 16
KC = IN_MATS * K
WID = OUT_MATS * N
R = B * T * M
IN_FEATURES = IN_MATS * M * K
OUT_FEATURES = OUT_MATS * M * N


def setup_inputs():
    s = mx_kscale(R).reshape(B, T, 1, M, 1)
    x = np.random.standard_normal((B, T, IN_MATS, M, K)) * s
    weight = np.random.standard_normal((OUT_MATS, IN_MATS, N, K)) / np.sqrt(KC)
    bias = np.random.standard_normal((OUT_MATS, M, N)) * 0.3
    g = np.random.standard_normal((B, T, OUT_MATS, M, N)) * np.exp2(np.random.randint(-12, 1, (B, T, 1, 1, 1))) / s
    return {"x": bf(x.reshape(B, T, IN_FEATURES)), "weight": bf(weight), "bias": bf(bias),
            "grad_out": bf(g.reshape(B, T, OUT_FEATURES))}


def reference(x, weight, bias, grad_out):
    xr = f64(x).reshape(B * T, IN_MATS, M, K).transpose(0, 2, 1, 3).reshape(R, KC)
    gr = f64(grad_out).reshape(B * T, OUT_MATS, M, N).transpose(0, 2, 1, 3).reshape(R, WID)
    gw = mxq(gr, 0, "e5m2").T @ mxq(xr, 0, "e4m3")
    return gw.reshape(OUT_MATS, N, IN_MATS, K).transpose(0, 2, 1, 3)

@@ -1,0 +1,132 @@
+from contextlib import ExitStack
+
+import concourse.mybir as mybir
+
+BF16 = mybir.dt.bfloat16
+F32 = mybir.dt.float32
+U32 = mybir.dt.uint32
+U8 = mybir.dt.uint8
+E4M3X4 = mybir.dt.float8_e4m3fn_x4
+E5M2X4 = mybir.dt.float8_e5m2_x4
+
+P = 128
+TOKENS = 512
+FEATURES = 4096
+COLS = 512
+FLOPS = 2 * COLS * COLS * TOKENS * 8
+BYTES = 2 * TOKENS * FEATURES * 2 + COLS * COLS * 4
+
+X_SPLIT = {0: ((0, 8), (8, 8), (16, 16)), 1: ((0, 32),), 2: ((0, 32),), 3: ((0, 32),)}
+G_SPLIT = {0: ((0, 16),), 1: ((0, 16),), 2: ((0, 16),), 3: ((0, 4), (4, 4), (8, 4), (12, 4))}
+INNER = {"x": 16, "g": 32}
+
+
+def tile_blocklinear_kernel(tc, x, weight, bias, grad_out, out):
+    nc = tc.nc
+    views = {
+        "x": x.flatten_outer_dims().rearrange("(a cl j) f -> cl j a f", cl=4, j=4),
+        "g": grad_out.flatten_outer_dims().rearrange("(a cl j) f -> cl j a f", cl=4, j=4),
+    }
+    out_rows = out.rearrange("(mt o) c n k -> mt (o c) (n k)", o=4)
+    fmt = {"x": E4M3X4, "g": E5M2X4}
+
+    with ExitStack() as ctx:
+        raw_pool = ctx.enter_context(tc.tile_pool(name="raw", bufs=1))
+        keep = ctx.enter_context(tc.tile_pool(name="keep", bufs=1))
+        stage = ctx.enter_context(tc.tile_pool(name="stage", bufs=6))
+        tail = ctx.enter_context(tc.tile_pool(name="tail", bufs=4))
+        psum = ctx.enter_context(tc.psum_pool(name="acc", bufs=1))
+
+        codes = {}
+        scales = {}
+        for op in ("x", "g"):
+            codes[op] = keep.tile([P, 8, COLS], U32, name="codes_%s" % op, align_bytes=64)
+            scales[op] = keep.tile([P, 8, COLS], U8, name="scales_%s" % op, align_bytes=64)
+        acc = [psum.tile([P, COLS], F32, name="acc%d" % mt) for mt in range(4)]
+
+        pieces = []
+        raw = {}
+        for cl in range(4):
+            for op, split in (("x", X_SPLIT), ("g", G_SPLIT)):
+                raw[(op, cl)] = raw_pool.tile([P, FEATURES], BF16, name="raw_%s%d" % (op, cl))
+                width = 8 * INNER[op]
+                for lo, n in split[cl]:
+                    pieces.append((op, cl, lo, n))
+                    for j in range(4):
+                        nc.sync.dma_start(
+                            out=raw[(op, cl)][j:P:4, lo * width : (lo + n) * width],
+                            in_=views[op][cl, j][:, lo * width : (lo + n) * width],
+                        )
+
+        def regroup(piece):
+            op, cl, lo, n = piece
+            inner = INNER[op]
+            width = 8 * inner
+            src = raw[(op, cl)][:, lo * width : (lo + n) * width]
+            halves = []
+            for h in range(2):
+                grouped = stage.tile([P, n * inner * 4], BF16, name="grouped", tag="grouped", align_bytes=64)
+                if h == 0:
+                    nc.vector.tensor_copy(
+                        out=grouped[:].rearrange("p (c q i t) -> p c q t i", c=n, q=inner // 4, i=4, t=4),
+                        in_=src.rearrange("p (c h t q i) -> p h c q t i", c=n, h=2, t=4, q=inner // 4, i=4)[:, h],
+                    )
+                else:
+                    nc.scalar.copy(
+                        out=grouped[:].rearrange("p (c k t) -> p c k t", c=n, k=inner, t=4),
+                        in_=src.rearrange("p (c h t k) -> p h c k t", c=n, h=2, t=4, k=inner)[:, h],
+                    )
+                halves.append(grouped)
+            return halves
+
+        def quantise(piece, halves):
+            op, cl, lo, n = piece
+            cols = slice(lo * INNER[op], (lo + n) * INNER[op])
+            for h in range(2):
+                nc.vector.quantize_mx(
+                    out=codes[op][:, 2 * cl + h, cols].bitcast(fmt[op]),
+                    scales=scales[op][:, 2 * cl + h, cols],
+                    in_=halves[h][:],
+                )
+
+        def multiply(cl, mt):
+            rows = slice(mt * P, (mt + 1) * P)
+            for h in range(2):
+                ps = 2 * cl + h
+                nc.tensor.matmul_mx(
+                    out=acc[mt][:],
+                    lhsT=codes["g"][:, ps, rows].bitcast(E5M2X4),
+                    lhsT_scale=scales["g"][:, ps, rows],
+                    rhs=codes["x"][:, ps, :].bitcast(E4M3X4),
+                    rhs_scale=scales["x"][:, ps, :],
+                    start=(ps == 0),
+                    stop=(ps == 7),
+                )
+
+        def finish(mt):
+            by_k = tail.tile([P, COLS], F32, name="by_k", tag="by_k", align_bytes=64)
+            nc.scalar.copy(
+                out=by_k[:].rearrange("p (k c) -> p k c", k=16),
+                in_=acc[mt][:].rearrange("p (c k) -> p k c", k=16),
+            )
+            flipped = tail.tile([P, COLS], F32, name="flipped", tag="flipped", align_bytes=64)
+            nc.vector.transpose(out=flipped[:], in_=by_k[:])
+            result = tail.tile([P, COLS], F32, name="result", tag="result", align_bytes=64)
+            nc.vector.tensor_copy(
+                out=result[:].rearrange("p (q i k) -> p q k i", q=8, i=4, k=16),
+                in_=flipped[:].rearrange("p (k q i) -> p q k i", k=16, q=8, i=4),
+            )
+            nc.sync.dma_start(out=out_rows[mt], in_=result[:])
+
+        waiting = None
+        for piece in pieces + [None]:
+            halves = regroup(piece) if piece is not None else None
+            if waiting is not None:
+                quantise(waiting[0], waiting[1])
+                op, cl, lo, n = waiting[0]
+                if op == "g":
+                    for mt in range(lo // 4, (lo + n) // 4):
+                        multiply(cl, mt)
+                        if cl == 3:
+                            finish(mt)
+            waiting = (piece, halves)

@@ -16,117 +16,167 @@ COLS = 512
 FLOPS = 2 * COLS * COLS * TOKENS * 8
 BYTES = 2 * TOKENS * FEATURES * 2 + COLS * COLS * 4
 
-X_SPLIT = {0: ((0, 8), (8, 8), (16, 16)), 1: ((0, 32),), 2: ((0, 32),), 3: ((0, 32),)}
-G_SPLIT = {0: ((0, 16),), 1: ((0, 16),), 2: ((0, 16),), 3: ((0, 4), (4, 4), (8, 4), (12, 4))}
+LOADS = (("x",0,0,4,),("x",0,4,4,),("x",0,8,8,),("x",0,16,16,),("x",1,0,16,),("x",1,16,16,),("g",0,0,16,),("x",2,0,32,),("g",1,0,16,),("x",3,0,32,),("g",2,0,16,),("g",3,0,8,),("g",3,8,8,),)
+PIECES = (("x",0,0,4,"VS",),("x",0,4,4,"VS",),("x",0,8,8,"VS",),("x",0,16,16,"VS",),("x",1,0,16,"VS",),("x",1,16,16,"VS",),("g",0,0,16,"VS",),("x",2,0,32,"VS",),("g",1,0,16,"VS",),("x",3,0,32,"VS",),("g",2,0,4,"VS",),("g",2,4,4,"VS",),("g",2,8,4,"VS",),("g",2,12,4,"VS",),("g",3,0,4,"VS",),("g",3,4,4,"VS",),("g",3,8,4,"VS",),("g",3,12,4,"VS",),)
 INNER = {"x": 16, "g": 32}
+DIRECT = (0,1,)
+LAG_E = (2,2,3,0,)
+LAG_T = (0,0,1,0,)
+LAG_P = (0,0,0,0,)
+ENG_E = ("S","S","S","S",)
+ENG_P = ("V","V","V","V",)
 
 
 def tile_blocklinear_kernel(tc, x, weight, bias, grad_out, out):
     nc = tc.nc
-    views = {
-        "x": x.flatten_outer_dims().rearrange("(a cl j) f -> cl j a f", cl=4, j=4),
-        "g": grad_out.flatten_outer_dims().rearrange("(a cl j) f -> cl j a f", cl=4, j=4),
-    }
+    x_view = x.flatten_outer_dims().rearrange("(a cl j) f -> cl j a f", cl=4, j=4)
+    g_view = grad_out.flatten_outer_dims().rearrange("(a cl j) (mt f) -> mt j a cl f", cl=4, j=4, mt=4)
     out_rows = out.rearrange("(mt o) c n k -> mt (o c) (n k)", o=4)
     fmt = {"x": E4M3X4, "g": E5M2X4}
 
     with ExitStack() as ctx:
+        ctx.enter_context(tc.manual_schedule())
         raw_pool = ctx.enter_context(tc.tile_pool(name="raw", bufs=1))
         keep = ctx.enter_context(tc.tile_pool(name="keep", bufs=1))
-        stage = ctx.enter_context(tc.tile_pool(name="stage", bufs=6))
+        stage = ctx.enter_context(tc.tile_pool(name="stage", bufs=8))
         tail = ctx.enter_context(tc.tile_pool(name="tail", bufs=4))
         psum = ctx.enter_context(tc.psum_pool(name="acc", bufs=1))
 
         codes = {}
         scales = {}
+        raw = {}
         for op in ("x", "g"):
             codes[op] = keep.tile([P, 8, COLS], U32, name="codes_%s" % op, align_bytes=64)
             scales[op] = keep.tile([P, 8, COLS], U8, name="scales_%s" % op, align_bytes=64)
+            for idx in range(4):
+                raw[(op, idx)] = raw_pool.tile([P, FEATURES], BF16, name="raw_%s%d" % (op, idx))
         acc = [psum.tile([P, COLS], F32, name="acc%d" % mt) for mt in range(4)]
 
-        pieces = []
-        raw = {}
-        for cl in range(4):
-            for op, split in (("x", X_SPLIT), ("g", G_SPLIT)):
-                raw[(op, cl)] = raw_pool.tile([P, FEATURES], BF16, name="raw_%s%d" % (op, cl))
-                width = 8 * INNER[op]
-                for lo, n in split[cl]:
-                    pieces.append((op, cl, lo, n))
-                    for j in range(4):
-                        nc.sync.dma_start(
-                            out=raw[(op, cl)][j:P:4, lo * width : (lo + n) * width],
-                            in_=views[op][cl, j][:, lo * width : (lo + n) * width],
-                        )
+        def copy_on(engine, dst_view, src_view):
+            if engine == "V":
+                nc.vector.tensor_copy(out=dst_view, in_=src_view)
+            else:
+                nc.scalar.copy(out=dst_view, in_=src_view)
+
+        for op, idx, lo, n in LOADS:
+            for j in range(4):
+                if op == "x":
+                    nc.sync.dma_start(
+                        out=raw[(op, idx)][j:P:4, lo * 128 : (lo + n) * 128],
+                        in_=x_view[idx, j][:, lo * 128 : (lo + n) * 128],
+                    )
+                else:
+                    nc.sync.dma_start(
+                        out=raw[(op, idx)][j:P:4, lo * 256 : (lo + n) * 256].rearrange("p (cl f) -> p cl f", f=1024),
+                        in_=g_view[idx, j][:, lo // 4 : (lo + n) // 4, :],
+                    )
 
         def regroup(piece):
-            op, cl, lo, n = piece
+            op, idx, lo, n, engines = piece
             inner = INNER[op]
             width = 8 * inner
-            src = raw[(op, cl)][:, lo * width : (lo + n) * width]
+            src = raw[(op, idx)][:, lo * width : (lo + n) * width]
             halves = []
             for h in range(2):
                 grouped = stage.tile([P, n * inner * 4], BF16, name="grouped", tag="grouped", align_bytes=64)
-                if h == 0:
-                    nc.vector.tensor_copy(
-                        out=grouped[:].rearrange("p (c q i t) -> p c q t i", c=n, q=inner // 4, i=4, t=4),
-                        in_=src.rearrange("p (c h t q i) -> p h c q t i", c=n, h=2, t=4, q=inner // 4, i=4)[:, h],
-                    )
-                else:
-                    nc.scalar.copy(
-                        out=grouped[:].rearrange("p (c k t) -> p c k t", c=n, k=inner, t=4),
-                        in_=src.rearrange("p (c h t k) -> p h c k t", c=n, h=2, t=4, k=inner)[:, h],
-                    )
+                copy_on(
+                    engines[h],
+                    grouped[:].rearrange("p (c q i t) -> p c q t i", c=n, q=inner // 4, i=4, t=4),
+                    src.rearrange("p (c h t q i) -> p h c q t i", c=n, h=2, t=4, q=inner // 4, i=4)[:, h],
+                )
                 halves.append(grouped)
             return halves
 
         def quantise(piece, halves):
-            op, cl, lo, n = piece
+            op, idx, lo, n, engines = piece
             cols = slice(lo * INNER[op], (lo + n) * INNER[op])
             for h in range(2):
                 nc.vector.quantize_mx(
-                    out=codes[op][:, 2 * cl + h, cols].bitcast(fmt[op]),
-                    scales=scales[op][:, 2 * cl + h, cols],
+                    out=codes[op][:, 2 * idx + h, cols].bitcast(fmt[op]),
+                    scales=scales[op][:, 2 * idx + h, cols],
                     in_=halves[h][:],
                 )
 
-        def multiply(cl, mt):
-            rows = slice(mt * P, (mt + 1) * P)
+        passes = [0, 0, 0, 0]
+
+        def multiply(mt, cl):
+            rows = slice(cl * P, (cl + 1) * P)
             for h in range(2):
-                ps = 2 * cl + h
                 nc.tensor.matmul_mx(
                     out=acc[mt][:],
-                    lhsT=codes["g"][:, ps, rows].bitcast(E5M2X4),
-                    lhsT_scale=scales["g"][:, ps, rows],
-                    rhs=codes["x"][:, ps, :].bitcast(E4M3X4),
-                    rhs_scale=scales["x"][:, ps, :],
-                    start=(ps == 0),
-                    stop=(ps == 7),
+                    lhsT=codes["g"][:, 2 * mt + h, rows].bitcast(E5M2X4),
+                    lhsT_scale=scales["g"][:, 2 * mt + h, rows],
+                    rhs=codes["x"][:, 2 * cl + h, :].bitcast(E4M3X4),
+                    rhs_scale=scales["x"][:, 2 * cl + h, :],
+                    start=(passes[mt] == 0),
+                    stop=(passes[mt] == 7),
+                )
+                passes[mt] += 1
+
+        emptied = {}
+        flipped = {}
+
+        def empty(mt):
+            emptied[mt] = tail.tile([P, COLS], F32, name="emptied", tag="emptied", align_bytes=64)
+            if mt in DIRECT:
+                copy_on(ENG_E[mt], emptied[mt][:], acc[mt][:])
+                for oq in range(4):
+                    nc.sync.dma_start(
+                        out=out[4 * mt + oq].rearrange("c n k -> n c k"),
+                        in_=emptied[mt][32 * oq : 32 * oq + 32, :].rearrange("p (c k) -> p c k", k=16),
+                    )
+            else:
+                copy_on(
+                    ENG_E[mt],
+                    emptied[mt][:].rearrange("p (k c) -> p k c", k=16),
+                    acc[mt][:].rearrange("p (c k) -> p k c", k=16),
                 )
 
-        def finish(mt):
-            by_k = tail.tile([P, COLS], F32, name="by_k", tag="by_k", align_bytes=64)
-            nc.scalar.copy(
-                out=by_k[:].rearrange("p (k c) -> p k c", k=16),
-                in_=acc[mt][:].rearrange("p (c k) -> p k c", k=16),
-            )
-            flipped = tail.tile([P, COLS], F32, name="flipped", tag="flipped", align_bytes=64)
-            nc.vector.transpose(out=flipped[:], in_=by_k[:])
-            result = tail.tile([P, COLS], F32, name="result", tag="result", align_bytes=64)
-            nc.vector.tensor_copy(
-                out=result[:].rearrange("p (q i k) -> p q k i", q=8, i=4, k=16),
-                in_=flipped[:].rearrange("p (k q i) -> p q k i", k=16, q=8, i=4),
+        def flip(mt):
+            flipped[mt] = tail.tile([P, COLS], F32, name="flipped", tag="flipped", align_bytes=64)
+            nc.vector.transpose(out=flipped[mt][:], in_=emptied[mt][:])
+
+        def store(mt):
+            result = tail.tile([P, COLS], F32, name="result", tag="result")
+            copy_on(
+                ENG_P[mt],
+                result[:].rearrange("p (q i k) -> p q k i", q=8, i=4, k=16),
+                flipped[mt][:].rearrange("p (k q i) -> p q k i", k=16, q=8, i=4),
             )
             nc.sync.dma_start(out=out_rows[mt], in_=result[:])
 
-        waiting = None
-        for piece in pieces + [None]:
-            halves = regroup(piece) if piece is not None else None
-            if waiting is not None:
-                quantise(waiting[0], waiting[1])
-                op, cl, lo, n = waiting[0]
-                if op == "g":
-                    for mt in range(lo // 4, (lo + n) // 4):
-                        multiply(cl, mt)
-                        if cl == 3:
-                            finish(mt)
-            waiting = (piece, halves)
+        x_groups = [0, 0, 0, 0]
+        g_ready = set()
+        issued = set()
+        closed_at = {}
+        grouped_of = {}
+        for s in range(len(PIECES) + 16):
+            if s < len(PIECES):
+                grouped_of[s] = regroup(PIECES[s])
+            if 1 <= s <= len(PIECES):
+                op, idx, lo, n, engines = PIECES[s - 1]
+                quantise(PIECES[s - 1], grouped_of[s - 1])
+                if op == "x":
+                    x_groups[idx] += n
+                else:
+                    for cl in range(lo // 4, (lo + n) // 4):
+                        g_ready.add((idx, cl))
+                for mt in range(4):
+                    for cl in range(4):
+                        if (mt, cl) not in issued and x_groups[cl] == 32 and (mt, cl) in g_ready:
+                            issued.add((mt, cl))
+                            multiply(mt, cl)
+                            if passes[mt] == 8:
+                                closed_at[mt] = s
+            for mt in range(4):
+                if mt not in closed_at:
+                    continue
+                since = s - closed_at[mt]
+                if since == LAG_E[mt]:
+                    empty(mt)
+                if mt in DIRECT:
+                    continue
+                if since == LAG_E[mt] + LAG_T[mt]:
+                    flip(mt)
+                if since == LAG_E[mt] + LAG_T[mt] + LAG_P[mt]:
+                    store(mt)

@@ -16,21 +16,23 @@ COLS = 512
 FLOPS = 2 * COLS * COLS * TOKENS * 8
 BYTES = 2 * TOKENS * FEATURES * 2 + COLS * COLS * 4
 
-LOADS = (("x",0,0,4,),("x",0,4,4,),("x",0,8,8,),("x",0,16,16,),("x",1,0,16,),("x",1,16,16,),("g",0,0,16,),("x",2,0,32,),("g",1,0,16,),("x",3,0,32,),("g",2,0,16,),("g",3,0,8,),("g",3,8,8,),)
-PIECES = (("x",0,0,4,"VS",),("x",0,4,4,"VS",),("x",0,8,8,"VS",),("x",0,16,16,"VS",),("x",1,0,16,"VS",),("x",1,16,16,"VS",),("g",0,0,16,"VS",),("x",2,0,32,"VS",),("g",1,0,16,"VS",),("x",3,0,32,"VS",),("g",2,0,4,"VS",),("g",2,4,4,"VS",),("g",2,8,4,"VS",),("g",2,12,4,"VS",),("g",3,0,4,"VS",),("g",3,4,4,"VS",),("g",3,8,4,"VS",),("g",3,12,4,"VS",),)
+LOADS = (("x",0,0,8,),("x",0,8,24,),("g",0,0,16,),("x",1,0,32,),("g",1,0,16,),("x",2,0,32,),("g",2,0,16,),("x",3,0,32,),("g",3,0,16,),)
+PIECES = (("x",0,0,8,"VS",),("x",0,8,24,"VS",),("g",0,0,16,"VS",),("x",1,0,32,"VS",),("g",1,0,16,"VS",),("x",2,0,32,"VS",),("g",2,0,16,"VS",),("x",3,0,32,"VS",),("g",3,0,4,"VS",),("g",3,4,4,"VS",),("g",3,8,4,"VS",),("g",3,12,4,"VS",),)
 INNER = {"x": 16, "g": 32}
-DIRECT = (0,1,)
-LAG_E = (2,2,3,0,)
-LAG_T = (0,0,1,0,)
+Q_ORDER = ((1,1,),(0,0,),)
+LAG_E = (2,1,0,0,)
+LAG_T = (1,1,1,0,)
 LAG_P = (0,0,0,0,)
 ENG_E = ("S","S","S","S",)
-ENG_P = ("V","V","V","V",)
+ENG_P = ("S","V","V","V",)
 
 
 def tile_blocklinear_kernel(tc, x, weight, bias, grad_out, out):
     nc = tc.nc
-    x_view = x.flatten_outer_dims().rearrange("(a cl j) f -> cl j a f", cl=4, j=4)
-    g_view = grad_out.flatten_outer_dims().rearrange("(a cl j) (mt f) -> mt j a cl f", cl=4, j=4, mt=4)
+    views = {
+        "x": x.flatten_outer_dims().rearrange("(a cl j) f -> cl j a f", cl=4, j=4),
+        "g": grad_out.flatten_outer_dims().rearrange("(a cl j) f -> cl j a f", cl=4, j=4),
+    }
     out_rows = out.rearrange("(mt o) c n k -> mt (o c) (n k)", o=4)
     fmt = {"x": E4M3X4, "g": E5M2X4}
 
@@ -48,8 +50,8 @@ def tile_blocklinear_kernel(tc, x, weight, bias, grad_out, out):
         for op in ("x", "g"):
             codes[op] = keep.tile([P, 8, COLS], U32, name="codes_%s" % op, align_bytes=64)
             scales[op] = keep.tile([P, 8, COLS], U8, name="scales_%s" % op, align_bytes=64)
-            for idx in range(4):
-                raw[(op, idx)] = raw_pool.tile([P, FEATURES], BF16, name="raw_%s%d" % (op, idx))
+            for cl in range(4):
+                raw[(op, cl)] = raw_pool.tile([P, FEATURES], BF16, name="raw_%s%d" % (op, cl))
         acc = [psum.tile([P, COLS], F32, name="acc%d" % mt) for mt in range(4)]
 
         def copy_on(engine, dst_view, src_view):
@@ -58,79 +60,92 @@ def tile_blocklinear_kernel(tc, x, weight, bias, grad_out, out):
             else:
                 nc.scalar.copy(out=dst_view, in_=src_view)
 
-        for op, idx, lo, n in LOADS:
+        for op, cl, lo, n in LOADS:
+            width = 8 * INNER[op]
             for j in range(4):
-                if op == "x":
-                    nc.sync.dma_start(
-                        out=raw[(op, idx)][j:P:4, lo * 128 : (lo + n) * 128],
-                        in_=x_view[idx, j][:, lo * 128 : (lo + n) * 128],
-                    )
-                else:
-                    nc.sync.dma_start(
-                        out=raw[(op, idx)][j:P:4, lo * 256 : (lo + n) * 256].rearrange("p (cl f) -> p cl f", f=1024),
-                        in_=g_view[idx, j][:, lo // 4 : (lo + n) // 4, :],
-                    )
+                nc.sync.dma_start(
+                    out=raw[(op, cl)][j:P:4, lo * width : (lo + n) * width],
+                    in_=views[op][cl, j][:, lo * width : (lo + n) * width],
+                )
+
+        grouped = {}
 
         def regroup(piece):
-            op, idx, lo, n, engines = piece
+            op, cl, lo, n, engines = piece
             inner = INNER[op]
             width = 8 * inner
-            src = raw[(op, idx)][:, lo * width : (lo + n) * width]
-            halves = []
+            src = raw[(op, cl)][:, lo * width : (lo + n) * width]
             for h in range(2):
-                grouped = stage.tile([P, n * inner * 4], BF16, name="grouped", tag="grouped", align_bytes=64)
-                copy_on(
-                    engines[h],
-                    grouped[:].rearrange("p (c q i t) -> p c q t i", c=n, q=inner // 4, i=4, t=4),
-                    src.rearrange("p (c h t q i) -> p h c q t i", c=n, h=2, t=4, q=inner // 4, i=4)[:, h],
-                )
-                halves.append(grouped)
-            return halves
-
-        def quantise(piece, halves):
-            op, idx, lo, n, engines = piece
-            cols = slice(lo * INNER[op], (lo + n) * INNER[op])
-            for h in range(2):
-                nc.vector.quantize_mx(
-                    out=codes[op][:, 2 * idx + h, cols].bitcast(fmt[op]),
-                    scales=scales[op][:, 2 * idx + h, cols],
-                    in_=halves[h][:],
-                )
+                if op == "x":
+                    if lo == 0:
+                        grouped[(op, cl, 0, h)] = stage.tile([P, 4 * COLS], BF16, name="grouped", tag="grouped", align_bytes=64)
+                    whole = grouped[(op, cl, 0, h)]
+                    copy_on(
+                        engines[h],
+                        whole[:, lo * 64 : (lo + n) * 64].rearrange("p (c q i t) -> p c q t i", c=n, q=4, i=4, t=4),
+                        src.rearrange("p (c h t q i) -> p h c q t i", c=n, h=2, t=4, q=4, i=4)[:, h],
+                    )
+                else:
+                    grouped[(op, cl, lo, h)] = stage.tile([P, n * 128], BF16, name="grouped", tag="grouped", align_bytes=64)
+                    copy_on(
+                        engines[h],
+                        grouped[(op, cl, lo, h)][:].rearrange("p (c q i t) -> p c q t i", c=n, q=8, i=4, t=4),
+                        src.rearrange("p (c h t q i) -> p h c q t i", c=n, h=2, t=4, q=8, i=4)[:, h],
+                    )
 
         passes = [0, 0, 0, 0]
+        x_ready = set()
+        g_ready = set()
+        issued = set()
+        closed_at = {}
 
-        def multiply(mt, cl):
-            rows = slice(cl * P, (cl + 1) * P)
-            for h in range(2):
-                nc.tensor.matmul_mx(
-                    out=acc[mt][:],
-                    lhsT=codes["g"][:, 2 * mt + h, rows].bitcast(E5M2X4),
-                    lhsT_scale=scales["g"][:, 2 * mt + h, rows],
-                    rhs=codes["x"][:, 2 * cl + h, :].bitcast(E4M3X4),
-                    rhs_scale=scales["x"][:, 2 * cl + h, :],
-                    start=(passes[mt] == 0),
-                    stop=(passes[mt] == 7),
-                )
-                passes[mt] += 1
+        def quantise(piece, h, s):
+            op, cl, lo, n, engines = piece
+            if op == "x":
+                if lo + n < 32:
+                    return
+                cols = slice(0, COLS)
+                source = grouped[(op, cl, 0, h)]
+                x_ready.add((cl, h))
+            else:
+                cols = slice(lo * 32, (lo + n) * 32)
+                source = grouped[(op, cl, lo, h)]
+                for mt in range(lo // 4, (lo + n) // 4):
+                    g_ready.add((cl, h, mt))
+            nc.vector.quantize_mx(
+                out=codes[op][:, 2 * cl + h, cols].bitcast(fmt[op]),
+                scales=scales[op][:, 2 * cl + h, cols],
+                in_=source[:],
+            )
+            for c2 in range(4):
+                for mt in range(4):
+                    key = (c2, h, mt)
+                    if key not in issued and (c2, h) in x_ready and key in g_ready:
+                        issued.add(key)
+                        rows = slice(mt * P, (mt + 1) * P)
+                        nc.tensor.matmul_mx(
+                            out=acc[mt][:],
+                            lhsT=codes["g"][:, 2 * c2 + h, rows].bitcast(E5M2X4),
+                            lhsT_scale=scales["g"][:, 2 * c2 + h, rows],
+                            rhs=codes["x"][:, 2 * c2 + h, :].bitcast(E4M3X4),
+                            rhs_scale=scales["x"][:, 2 * c2 + h, :],
+                            start=(passes[mt] == 0),
+                            stop=(passes[mt] == 7),
+                        )
+                        passes[mt] += 1
+                        if passes[mt] == 8:
+                            closed_at[mt] = s
 
         emptied = {}
         flipped = {}
 
         def empty(mt):
             emptied[mt] = tail.tile([P, COLS], F32, name="emptied", tag="emptied", align_bytes=64)
-            if mt in DIRECT:
-                copy_on(ENG_E[mt], emptied[mt][:], acc[mt][:])
-                for oq in range(4):
-                    nc.sync.dma_start(
-                        out=out[4 * mt + oq].rearrange("c n k -> n c k"),
-                        in_=emptied[mt][32 * oq : 32 * oq + 32, :].rearrange("p (c k) -> p c k", k=16),
-                    )
-            else:
-                copy_on(
-                    ENG_E[mt],
-                    emptied[mt][:].rearrange("p (k c) -> p k c", k=16),
-                    acc[mt][:].rearrange("p (c k) -> p k c", k=16),
-                )
+            copy_on(
+                ENG_E[mt],
+                emptied[mt][:].rearrange("p (k c) -> p k c", k=16),
+                acc[mt][:].rearrange("p (c k) -> p k c", k=16),
+            )
 
         def flip(mt):
             flipped[mt] = tail.tile([P, COLS], F32, name="flipped", tag="flipped", align_bytes=64)
@@ -145,37 +160,18 @@ def tile_blocklinear_kernel(tc, x, weight, bias, grad_out, out):
             )
             nc.sync.dma_start(out=out_rows[mt], in_=result[:])
 
-        x_groups = [0, 0, 0, 0]
-        g_ready = set()
-        issued = set()
-        closed_at = {}
-        grouped_of = {}
-        for s in range(len(PIECES) + 16):
+        for s in range(len(PIECES) + 20):
             if s < len(PIECES):
-                grouped_of[s] = regroup(PIECES[s])
-            if 1 <= s <= len(PIECES):
-                op, idx, lo, n, engines = PIECES[s - 1]
-                quantise(PIECES[s - 1], grouped_of[s - 1])
-                if op == "x":
-                    x_groups[idx] += n
-                else:
-                    for cl in range(lo // 4, (lo + n) // 4):
-                        g_ready.add((idx, cl))
-                for mt in range(4):
-                    for cl in range(4):
-                        if (mt, cl) not in issued and x_groups[cl] == 32 and (mt, cl) in g_ready:
-                            issued.add((mt, cl))
-                            multiply(mt, cl)
-                            if passes[mt] == 8:
-                                closed_at[mt] = s
+                regroup(PIECES[s])
+            for h, lag in Q_ORDER:
+                if 0 <= s - lag < len(PIECES):
+                    quantise(PIECES[s - lag], h, s)
             for mt in range(4):
                 if mt not in closed_at:
                     continue
                 since = s - closed_at[mt]
                 if since == LAG_E[mt]:
                     empty(mt)
-                if mt in DIRECT:
-                    continue
                 if since == LAG_E[mt] + LAG_T[mt]:
                     flip(mt)
                 if since == LAG_E[mt] + LAG_T[mt] + LAG_P[mt]:

@@ -82,15 +82,15 @@ def tile_blocklinear_kernel(tc, x, weight, bias, grad_out, out):
                     whole = grouped[(op, cl, 0, h)]
                     copy_on(
                         engines[h],
-                        whole[:, lo * 64 : (lo + n) * 64].rearrange("p (c q i t) -> p c q t i", c=n, q=4, i=4, t=4),
-                        src.rearrange("p (c h t q i) -> p h c q t i", c=n, h=2, t=4, q=4, i=4)[:, h],
+                        whole[:, lo * 64 : (lo + n) * 64].rearrange("p (c q i t) -> p c q t i", c=n, q=2, i=8, t=4),
+                        src.rearrange("p (c h t q i) -> p h c q t i", c=n, h=2, t=4, q=2, i=8)[:, h],
                     )
                 else:
                     grouped[(op, cl, lo, h)] = stage.tile([P, n * 128], BF16, name="grouped", tag="grouped", align_bytes=64)
                     copy_on(
                         engines[h],
-                        grouped[(op, cl, lo, h)][:].rearrange("p (c q i t) -> p c q t i", c=n, q=8, i=4, t=4),
-                        src.rearrange("p (c h t q i) -> p h c q t i", c=n, h=2, t=4, q=8, i=4)[:, h],
+                        grouped[(op, cl, lo, h)][:].rearrange("p (c q i t) -> p c q t i", c=n, q=4, i=8, t=4),
+                        src.rearrange("p (c h t q i) -> p h c q t i", c=n, h=2, t=4, q=4, i=8)[:, h],
                     )
 
         passes = [0, 0, 0, 0]

@@ -16,8 +16,8 @@ COLS = 512
 FLOPS = 2 * COLS * COLS * TOKENS * 8
 BYTES = 2 * TOKENS * FEATURES * 2 + COLS * COLS * 4
 
-LOADS = (("x",0,0,8,),("x",0,8,24,),("g",0,0,16,),("x",1,0,32,),("g",1,0,16,),("x",2,0,32,),("g",2,0,16,),("x",3,0,32,),("g",3,0,16,),)
-PIECES = (("x",0,0,8,"VS",),("x",0,8,24,"VS",),("g",0,0,16,"VS",),("x",1,0,32,"VS",),("g",1,0,16,"VS",),("x",2,0,32,"VS",),("g",2,0,16,"VS",),("x",3,0,32,"VS",),("g",3,0,4,"VS",),("g",3,4,4,"VS",),("g",3,8,4,"VS",),("g",3,12,4,"VS",),)
+LOADS = (("x",0,0,16,),("x",0,16,16,),("g",0,0,16,),("x",1,0,32,),("g",1,0,16,),("x",2,0,32,),("g",2,0,16,),("x",3,0,32,),("g",3,0,16,),)
+PIECES = (("x",0,0,16,"VS",),("x",0,16,16,"VS",),("g",0,0,16,"VS",),("x",1,0,32,"VS",),("g",1,0,16,"VS",),("x",2,0,32,"VS",),("g",2,0,16,"VS",),("x",3,0,32,"VS",),("g",3,0,4,"VS",),("g",3,4,4,"VS",),("g",3,8,4,"VS",),("g",3,12,4,"VS",),)
 INNER = {"x": 16, "g": 32}
 Q_ORDER = ((1,1,),(0,0,),)
 LAG_E = (2,1,0,0,)

from contextlib import ExitStack

import concourse.mybir as mybir

BF16 = mybir.dt.bfloat16
F32 = mybir.dt.float32
U32 = mybir.dt.uint32
U8 = mybir.dt.uint8
E4M3X4 = mybir.dt.float8_e4m3fn_x4
E5M2X4 = mybir.dt.float8_e5m2_x4

P = 128
TOKENS = 512
FEATURES = 4096
COLS = 512
FLOPS = 2 * COLS * COLS * TOKENS * 8
BYTES = 2 * TOKENS * FEATURES * 2 + COLS * COLS * 4

LOADS = (("x",0,0,16,),("x",0,16,16,),("g",0,0,16,),("x",1,0,32,),("g",1,0,16,),("x",2,0,32,),("g",2,0,16,),("x",3,0,32,),("g",3,0,16,),)
PIECES = (("x",0,0,16,"VS",),("x",0,16,16,"VS",),("g",0,0,16,"VS",),("x",1,0,32,"VS",),("g",1,0,16,"VS",),("x",2,0,32,"VS",),("g",2,0,16,"VS",),("x",3,0,32,"VS",),("g",3,0,4,"VS",),("g",3,4,4,"VS",),("g",3,8,4,"VS",),("g",3,12,4,"VS",),)
INNER = {"x": 16, "g": 32}
Q_ORDER = ((1,1,),(0,0,),)
LAG_E = (2,1,0,0,)
LAG_T = (1,1,1,0,)
LAG_P = (0,0,0,0,)
ENG_E = ("S","S","S","S",)
ENG_P = ("S","V","V","V",)


def tile_blocklinear_kernel(tc, x, weight, bias, grad_out, out):
    nc = tc.nc
    views = {
        "x": x.flatten_outer_dims().rearrange("(a cl j) f -> cl j a f", cl=4, j=4),
        "g": grad_out.flatten_outer_dims().rearrange("(a cl j) f -> cl j a f", cl=4, j=4),
    }
    out_rows = out.rearrange("(mt o) c n k -> mt (o c) (n k)", o=4)
    fmt = {"x": E4M3X4, "g": E5M2X4}

    with ExitStack() as ctx:
        ctx.enter_context(tc.manual_schedule())
        raw_pool = ctx.enter_context(tc.tile_pool(name="raw", bufs=1))
        keep = ctx.enter_context(tc.tile_pool(name="keep", bufs=1))
        stage = ctx.enter_context(tc.tile_pool(name="stage", bufs=8))
        tail = ctx.enter_context(tc.tile_pool(name="tail", bufs=4))
        psum = ctx.enter_context(tc.psum_pool(name="acc", bufs=1))

        codes = {}
        scales = {}
        raw = {}
        for op in ("x", "g"):
            codes[op] = keep.tile([P, 8, COLS], U32, name="codes_%s" % op, align_bytes=64)
            scales[op] = keep.tile([P, 8, COLS], U8, name="scales_%s" % op, align_bytes=64)
            for cl in range(4):
                raw[(op, cl)] = raw_pool.tile([P, FEATURES], BF16, name="raw_%s%d" % (op, cl))
        acc = [psum.tile([P, COLS], F32, name="acc%d" % mt) for mt in range(4)]

        def copy_on(engine, dst_view, src_view):
            if engine == "V":
                nc.vector.tensor_copy(out=dst_view, in_=src_view)
            else:
                nc.scalar.copy(out=dst_view, in_=src_view)

        for op, cl, lo, n in LOADS:
            width = 8 * INNER[op]
            for j in range(4):
                nc.sync.dma_start(
                    out=raw[(op, cl)][j:P:4, lo * width : (lo + n) * width],
                    in_=views[op][cl, j][:, lo * width : (lo + n) * width],
                )

        grouped = {}

        def regroup(piece):
            op, cl, lo, n, engines = piece
            inner = INNER[op]
            width = 8 * inner
            src = raw[(op, cl)][:, lo * width : (lo + n) * width]
            for h in range(2):
                if op == "x":
                    if lo == 0:
                        grouped[(op, cl, 0, h)] = stage.tile([P, 4 * COLS], BF16, name="grouped", tag="grouped", align_bytes=64)
                    whole = grouped[(op, cl, 0, h)]
                    copy_on(
                        engines[h],
                        whole[:, lo * 64 : (lo + n) * 64].rearrange("p (c q i t) -> p c q t i", c=n, q=2, i=8, t=4),
                        src.rearrange("p (c h t q i) -> p h c q t i", c=n, h=2, t=4, q=2, i=8)[:, h],
                    )
                else:
                    grouped[(op, cl, lo, h)] = stage.tile([P, n * 128], BF16, name="grouped", tag="grouped", align_bytes=64)
                    copy_on(
                        engines[h],
                        grouped[(op, cl, lo, h)][:].rearrange("p (c q i t) -> p c q t i", c=n, q=4, i=8, t=4),
                        src.rearrange("p (c h t q i) -> p h c q t i", c=n, h=2, t=4, q=4, i=8)[:, h],
                    )

        passes = [0, 0, 0, 0]
        x_ready = set()
        g_ready = set()
        issued = set()
        closed_at = {}

        def quantise(piece, h, s):
            op, cl, lo, n, engines = piece
            if op == "x":
                if lo + n < 32:
                    return
                cols = slice(0, COLS)
                source = grouped[(op, cl, 0, h)]
                x_ready.add((cl, h))
            else:
                cols = slice(lo * 32, (lo + n) * 32)
                source = grouped[(op, cl, lo, h)]
                for mt in range(lo // 4, (lo + n) // 4):
                    g_ready.add((cl, h, mt))
            nc.vector.quantize_mx(
                out=codes[op][:, 2 * cl + h, cols].bitcast(fmt[op]),
                scales=scales[op][:, 2 * cl + h, cols],
                in_=source[:],
            )
            for c2 in range(4):
                for mt in range(4):
                    key = (c2, h, mt)
                    if key not in issued and (c2, h) in x_ready and key in g_ready:
                        issued.add(key)
                        rows = slice(mt * P, (mt + 1) * P)
                        nc.tensor.matmul_mx(
                            out=acc[mt][:],
                            lhsT=codes["g"][:, 2 * c2 + h, rows].bitcast(E5M2X4),
                            lhsT_scale=scales["g"][:, 2 * c2 + h, rows],
                            rhs=codes["x"][:, 2 * c2 + h, :].bitcast(E4M3X4),
                            rhs_scale=scales["x"][:, 2 * c2 + h, :],
                            start=(passes[mt] == 0),
                            stop=(passes[mt] == 7),
                        )
                        passes[mt] += 1
                        if passes[mt] == 8:
                            closed_at[mt] = s

        emptied = {}
        flipped = {}

        def empty(mt):
            emptied[mt] = tail.tile([P, COLS], F32, name="emptied", tag="emptied", align_bytes=64)
            copy_on(
                ENG_E[mt],
                emptied[mt][:].rearrange("p (k c) -> p k c", k=16),
                acc[mt][:].rearrange("p (c k) -> p k c", k=16),
            )

        def flip(mt):
            flipped[mt] = tail.tile([P, COLS], F32, name="flipped", tag="flipped", align_bytes=64)
            nc.vector.transpose(out=flipped[mt][:], in_=emptied[mt][:])

        def store(mt):
            result = tail.tile([P, COLS], F32, name="result", tag="result")
            copy_on(
                ENG_P[mt],
                result[:].rearrange("p (q i k) -> p q k i", q=8, i=4, k=16),
                flipped[mt][:].rearrange("p (k q i) -> p q k i", k=16, q=8, i=4),
            )
            nc.sync.dma_start(out=out_rows[mt], in_=result[:])

        for s in range(len(PIECES) + 20):
            if s < len(PIECES):
                regroup(PIECES[s])
            for h, lag in Q_ORDER:
                if 0 <= s - lag < len(PIECES):
                    quantise(PIECES[s - lag], h, s)
            for mt in range(4):
                if mt not in closed_at:
                    continue
                since = s - closed_at[mt]
                if since == LAG_E[mt]:
                    empty(mt)
                if since == LAG_E[mt] + LAG_T[mt]:
                    flip(mt)
                if since == LAG_E[mt] + LAG_T[mt] + LAG_P[mt]:
                    store(mt)
